import numpy as np
import ml_dtypes


def mxq(x, axis, fmt="e4m3"):
    dtype, down = {"e4m3": (ml_dtypes.float8_e4m3fn, 7), "e5m2": (ml_dtypes.float8_e5m2, 14)}[fmt]
    v = np.moveaxis(np.asarray(x, np.float32).astype(ml_dtypes.bfloat16).astype(np.float64), axis, -1)
    blocks = v.reshape(v.shape[:-1] + (-1, 32))
    amax = np.abs(blocks).max(-1, keepdims=True)
    byte = np.maximum(np.where(amax > 0, np.frexp(amax)[1] - 1 + 127, 0) - down, 1)
    scale = np.exp2(byte - 127.0)
    codes = (blocks / scale).astype(np.float32).astype(dtype).astype(np.float64)
    return np.moveaxis((codes * scale).reshape(v.shape), -1, axis)


WIDE = False


def mx_kscale(k):
    if not WIDE:
        return np.ones(k)
    levels = np.array([10, -10, 5, -5, 0])
    if k % 512:
        return np.exp2(np.random.permutation(np.resize(levels, k // 32))).repeat(32)
    a = np.empty((k // 512, 16))
    for p in range(k // 512):
        a[p, :8] = np.random.permutation(np.resize(levels, 8))
        for g in range(8):
            far = levels[np.abs(levels - a[p, g]) >= 10]
            a[p, g + 8] = far[np.random.randint(len(far))]
    return np.exp2(a.ravel()).repeat(32)


BF16 = ml_dtypes.bfloat16


def bf(x):
    return np.asarray(x, np.float32).astype(BF16)


def f64(x):
    return np.asarray(x).astype(np.float64)


B, K, NH, N = 8192, 1024, 512, 128
EPSILON = 0.1


def setup_inputs():
    s = mx_kscale(K)
    g = 1.0 / np.mean(1.0 / s)
    return {"x": bf(np.random.standard_normal((B, K)) * s),
            "y": bf(np.random.standard_normal((B, N)) * 12.0 / np.sqrt(K) * g),
            "beta": bf(np.random.random((K, N)) * 1.7 / np.sqrt(K) / s[:, None]),
            "bias_lin": bf(np.random.standard_normal(N) * 0.1),
            "W1": bf(-np.random.random((NH, K)) * 1.7 / np.sqrt(K) / s[None, :]),
            "W2": bf(np.random.random((N, NH)) * (0.5 + np.random.random((N, 1))) * 2.0 / NH**2),
            "bias1": bf(np.random.standard_normal(NH) * 0.1),
            "bias2": bf(np.random.standard_normal(N) * 0.1),
            "adv": 1}


def reference(x, y, beta, bias_lin, W1, W2, bias1, bias2, adv):
    xq = mxq(f64(x), 1, "e4m3")
    lin = (xq @ mxq(f64(beta), 0, "e4m3")) + f64(bias_lin)
    if adv:
        beta_norm = np.sum(np.abs(f64(beta)), axis=0)
        lin = lin - EPSILON * f64(y) * beta_norm
    if adv:
        one = NH * np.sum(f64(W2), axis=1) + f64(bias2)
        one = np.broadcast_to(one, lin.shape)
    else:
        h = np.maximum((xq @ mxq(f64(W1), 1, "e4m3").T) + f64(bias1), 0.0)
        one = (mxq(h, 1, "e4m3") @ mxq(f64(W2), 1, "e4m3").T) + f64(bias2)
    return lin + one

@@ -1,0 +1,213 @@
+from contextlib import ExitStack
+
+import concourse.mybir as mybir
+from concourse.masks import make_identity
+
+F32 = mybir.dt.float32
+BF16 = mybir.dt.bfloat16
+U32 = mybir.dt.uint32
+U8 = mybir.dt.uint8
+FP8X4 = mybir.dt.float8_e4m3fn_x4
+ADD = mybir.AluOpType.add
+MULT = mybir.AluOpType.mult
+ACT = mybir.ActivationFunctionType
+
+P = 128
+B, K, N, NH = 8192, 1024, 128, 512
+NT = B // P
+GT = 4
+NG = NT // GT
+FLOPS = 2 * B * K * N
+BYTES = 2 * (B * K + B * N + K * N + N * NH + 2 * N) + 4 * B * N
+
+X_CHUNKS = [4,4,4,4,4,4,4,4,4,4,4,4,4,4,4,4]
+Y_BEFORE = [1,3,6,10]
+LAG_Q, LAG_M, LAG_E = 1, 2, 3
+Y_HEAD = 2
+ADD_ENGINE = "gpsimd"
+GRP_BUFS = 3
+COD_BUFS = 3
+XT_BUFS = 5
+LAST_Q_PARTS = 1
+
+
+def tile_advresnet_t_kernel(tc, x, y, beta, bias_lin, W1, W2, bias1, bias2, adv, out):
+    assert adv == 1
+    nc = tc.nc
+    with ExitStack() as ctx:
+        ctx.enter_context(tc.manual_schedule())
+        res = ctx.enter_context(tc.tile_pool(name="res", bufs=1))
+        grp_pool = ctx.enter_context(tc.tile_pool(name="grp", bufs=GRP_BUFS))
+        cod_pool = ctx.enter_context(tc.tile_pool(name="cod", bufs=COD_BUFS))
+        ps_c = ctx.enter_context(tc.psum_pool(name="psc", bufs=1))
+        ps_x = ctx.enter_context(tc.psum_pool(name="psx", bufs=XT_BUFS))
+        ps_o = ctx.enter_context(tc.psum_pool(name="pso", bufs=7 - XT_BUFS))
+
+        x_v = x.rearrange("(p t) k -> p t k", t=NT)
+        y_v = y.rearrange("(p t) j -> p t j", t=NT)
+        o_v = out.rearrange("(p t) j -> p t j", t=NT)
+
+        w2 = res.tile([P, NH], BF16, name="w2")
+        nc.scalar.dma_start(out=w2[:], in_=W2)
+        brows = res.tile([P, N], BF16, name="brows")
+        nc.vector.memset(brows[:], 0.0)
+        nc.scalar.dma_start(out=brows[0:1, :], in_=bias_lin.rearrange("(o n) -> o n", o=1))
+        nc.scalar.dma_start(out=brows[1:2, :], in_=bias2.rearrange("(o n) -> o n", o=1))
+
+        braw = res.tile([P, 8 * N], BF16, name="braw")
+        nc.sync.dma_start(
+            out=braw[:].rearrange("p (g c) -> p g c", g=2),
+            in_=beta.rearrange("(g p t) j -> p g (t j)", g=2, p=P, t=4),
+        )
+        x_tiles = []
+        x_of = []
+        y_tiles = []
+        s = 0
+        for i, c in enumerate(X_CHUNKS):
+            for yi, b in enumerate(Y_BEFORE):
+                if b == i:
+                    y_sb = res.tile([P, 16 * N], BF16, name="y%d" % yi)
+                    nc.sync.dma_start(out=y_sb[:], in_=y_v[:, 16 * yi : 16 * yi + 16, :].rearrange("p t j -> p (t j)"))
+                    y_tiles.append(y_sb)
+            x_sb = res.tile([P, c * K], BF16, name="x%d" % i)
+            nc.sync.dma_start(out=x_sb[:], in_=x_v[:, s : s + c, :].rearrange("p t k -> p (t k)"))
+            x_tiles.append(x_sb)
+            for r in range(c):
+                x_of.append((i, r))
+            s += c
+        assert s == NT
+
+        ident = res.tile([P, P], F32, name="ident")
+        make_identity(nc, ident[:])
+        ones_f = res.tile([P, P], F32, name="ones_f")
+        nc.vector.memset(ones_f[:], 1.0)
+        ones_b = res.tile([P, P], BF16, name="ones_b")
+        nc.vector.memset(ones_b[:], 1.0)
+        warm = res.tile([P, 1], F32, name="warm")
+        nc.vector.memset(warm[:], 0.0)
+        nc.scalar.activation(out=warm[:], in_=warm[:], func=ACT.Abs)
+
+        absb = res.tile([P, 8 * N], BF16, name="absb")
+        nc.scalar.activation(out=absb[:], in_=braw[:], func=ACT.Abs)
+        w2junk = res.tile([P, NH], F32, name="w2junk")
+        w2s = res.tile([P, 1], F32, name="w2s")
+        nc.scalar.activation(out=w2junk[:], in_=w2[:], func=ACT.Copy, scale=float(NH), accum_out=w2s[:])
+        bgrp = res.tile([P, 8 * N], BF16, name="bgrp", align_bytes=64)
+        nc.vector.tensor_copy(
+            out=bgrp[:].rearrange("p (g j t) -> p g j t", g=2, t=4),
+            in_=braw[:].rearrange("p (g t j) -> p g j t", g=2, t=4),
+        )
+        rhs_c = res.tile([P, N], F32, name="rhs_c")
+        nc.vector.scalar_tensor_tensor(
+            out=rhs_c[:], in0=ident[:], scalar=w2s[:, 0:1], in1=brows[:], op0=MULT, op1=ADD
+        )
+        cst = ps_c.tile([P, GT * N], F32, name="cst")
+        for a in range(8):
+            nc.tensor.matmul(
+                out=cst[:, 0:N], lhsT=ones_b[:], rhs=absb[:, a * N : (a + 1) * N], start=(a == 0), stop=(a == 7)
+            )
+        c_sb = res.tile([P, N], F32, name="c_sb")
+
+        def emit_c():
+            c_ps = ps_o.tile([P, GT * N], F32, name="ops")
+            nc.tensor.matmul(out=c_ps[:, 0:N], lhsT=ones_f[:], rhs=rhs_c[:], start=True, stop=True)
+            nc.scalar.copy(out=c_sb[:], in_=c_ps[:, 0:N])
+
+        bcod = res.tile([P, 2 * N], U32, name="bcod", align_bytes=64)
+        bscl = res.tile([P, 2 * N], U8, name="bscl", align_bytes=64)
+        nc.vector.quantize_mx(out=bcod[:].bitcast(FP8X4), scales=bscl[:], in_=bgrp[:])
+
+        grp_t = {}
+        cod_t = {}
+        ops_t = {}
+        o_chunks = [res.tile([P, 2 * GT * N], F32, name="o%d" % ci) for ci in range(NG // 2)]
+        o_tiles = [o_chunks[g // 2][:, (g % 2) * GT * N : (g % 2 + 1) * GT * N] for g in range(NG)]
+        add_eng = nc.gpsimd if ADD_ENGINE == "gpsimd" else nc.vector
+
+        def emit_transposes(g):
+            grp = grp_pool.tile([P, GT * K], BF16, name="grp", align_bytes=64)
+            grp_t[g] = grp
+            for tt in range(GT):
+                i, r = x_of[g * GT + tt]
+                xw = x_tiles[i][:, r * K : (r + 1) * K].bitcast(F32)
+                xt = ps_x.tile([P, 4, P], F32, name="xt")
+                for w in range(4):
+                    g0 = (w // 2) * 2 * P
+                    nc.tensor.transpose(xt[:, w, :], xw[:, g0 + w % 2 : g0 + 2 * P : 2], ident[:])
+                dst = grp[:, tt * K : (tt + 1) * K].bitcast(F32).rearrange("p (g r u) -> p g r u", g=2, u=2)
+                nc.scalar.copy(out=dst, in_=xt[:].rearrange("p (g u) r -> p g r u", u=2))
+
+        def emit_quant(g):
+            cod = cod_pool.tile([P, GT * 2 * P], U32, name="cod", align_bytes=64)
+            scl = cod_pool.tile([P, GT * 2 * P], U8, name="scl", align_bytes=64)
+            cod_t[g] = (cod, scl)
+            parts = LAST_Q_PARTS if g == NG - 1 else 1
+            wq = GT * 2 * P // parts
+            for h in range(parts):
+                nc.vector.quantize_mx(
+                    out=cod[:, h * wq : (h + 1) * wq].bitcast(FP8X4),
+                    scales=scl[:, h * wq : (h + 1) * wq],
+                    in_=grp_t[g][:, 4 * h * wq : 4 * (h + 1) * wq],
+                )
+
+        def emit_mx(g):
+            cod, scl = cod_t[g]
+            ops = ps_o.tile([P, GT * N], F32, name="ops")
+            ops_t[g] = ops
+            for tt in range(GT):
+                for h in range(2):
+                    cs = slice((2 * tt + h) * P, (2 * tt + h + 1) * P)
+                    nc.tensor.matmul_mx(
+                        out=ops[:, tt * N : (tt + 1) * N],
+                        lhsT=cod[:, cs].bitcast(FP8X4),
+                        lhsT_scale=scl[:, cs],
+                        rhs=bcod[:, h * N : (h + 1) * N].bitcast(FP8X4),
+                        rhs_scale=bscl[:, h * N : (h + 1) * N],
+                        start=(h == 0),
+                        stop=(h == 1),
+                    )
+
+        def emit_y_mul(g):
+            t0 = (g % 4) * GT
+            nc.vector.scalar_tensor_tensor(
+                out=o_tiles[g].rearrange("p (t j) -> p t j", j=N),
+                in0=y_tiles[g // 4][:, t0 * N : (t0 + GT) * N].rearrange("p (t j) -> p t j", j=N),
+                scalar=-0.1,
+                in1=cst[:, 0:N].unsqueeze(1).to_broadcast([P, GT, N]),
+                op0=MULT,
+                op1=MULT,
+            )
+
+        def emit_y_add(g):
+            o3 = o_tiles[g].rearrange("p (t j) -> p t j", j=N)
+            add_eng.tensor_tensor(out=o3, in0=o3, in1=c_sb[:].unsqueeze(1).to_broadcast([P, GT, N]), op=ADD)
+
+        def emit_epilogue(g):
+            nc.vector.tensor_tensor(out=o_tiles[g], in0=ops_t[g][:], in1=o_tiles[g], op=ADD)
+            if g >= NG - 2:
+                nc.sync.dma_start(out=o_v[:, g * GT : (g + 1) * GT, :].rearrange("p t j -> p (t j)"), in_=o_tiles[g])
+            elif g % 2 == 1:
+                t0 = (g - 1) * GT
+                nc.sync.dma_start(
+                    out=o_v[:, t0 : t0 + 2 * GT, :].rearrange("p t j -> p (t j)"), in_=o_chunks[g // 2][:]
+                )
+
+        for g in range(Y_HEAD):
+            emit_y_mul(g)
+        for g in range(NG + LAG_E):
+            if g < NG:
+                emit_transposes(g)
+            if g == 0:
+                emit_c()
+                for h in range(Y_HEAD):
+                    emit_y_add(h)
+            if 0 <= g - LAG_M < NG:
+                emit_mx(g - LAG_M)
+            if 0 <= g - LAG_E < NG:
+                emit_epilogue(g - LAG_E)
+            if g + Y_HEAD < NG:
+                emit_y_mul(g + Y_HEAD)
+            if 0 <= g - LAG_Q < NG:
+                emit_quant(g - LAG_Q)
+            if g + Y_HEAD < NG:
+                emit_y_add(g + Y_HEAD)

@@ -10,25 +10,26 @@ U8 = mybir.dt.uint8
 FP8X4 = mybir.dt.float8_e4m3fn_x4
 ADD = mybir.AluOpType.add
 MULT = mybir.AluOpType.mult
-ACT = mybir.ActivationFunctionType
+MAX = mybir.AluOpType.max
+AX = mybir.AxisListType.X
 
 P = 128
 B, K, N, NH = 8192, 1024, 128, 512
 NT = B // P
 GT = 4
-NG = NT // GT
 FLOPS = 2 * B * K * N
 BYTES = 2 * (B * K + B * N + K * N + N * NH + 2 * N) + 4 * B * N
 
-X_CHUNKS = [4,4,4,4,4,4,4,4,4,4,4,4,4,4,4,4]
-Y_BEFORE = [1,3,6,10]
+X_CHUNKS = [1, 1, 2] + [4] * 15
+Y_BEFORE = {2: 0, 5: 1, 8: 2, 11: 3}
+BETA_AT = 1
+GROUPS = [4] * 15 + [2, 1, 1]
+PERM = (3,)
+NG = len(GROUPS)
+STARTS = [sum(GROUPS[:g]) for g in range(NG)]
 LAG_Q, LAG_M, LAG_E = 1, 2, 3
-Y_HEAD = 2
-ADD_ENGINE = "gpsimd"
-GRP_BUFS = 3
-COD_BUFS = 3
 XT_BUFS = 5
-LAST_Q_PARTS = 1
+Y_COUNT = {1: 2, 2: 2}
 
 
 def tile_advresnet_t_kernel(tc, x, y, beta, bias_lin, W1, W2, bias1, bias2, adv, out):
@@ -37,8 +38,9 @@ def tile_advresnet_t_kernel(tc, x, y, beta, bias_lin, W1, W2, bias1, bias2, adv,
     with ExitStack() as ctx:
         ctx.enter_context(tc.manual_schedule())
         res = ctx.enter_context(tc.tile_pool(name="res", bufs=1))
-        grp_pool = ctx.enter_context(tc.tile_pool(name="grp", bufs=GRP_BUFS))
-        cod_pool = ctx.enter_context(tc.tile_pool(name="cod", bufs=COD_BUFS))
+        grp_pool = ctx.enter_context(tc.tile_pool(name="grp", bufs=3))
+        cod_pool = ctx.enter_context(tc.tile_pool(name="cod", bufs=3))
+        perm_pool = ctx.enter_context(tc.tile_pool(name="perm", bufs=3))
         ps_c = ctx.enter_context(tc.psum_pool(name="psc", bufs=1))
         ps_x = ctx.enter_context(tc.psum_pool(name="psx", bufs=XT_BUFS))
         ps_o = ctx.enter_context(tc.psum_pool(name="pso", bufs=7 - XT_BUFS))
@@ -47,34 +49,33 @@ def tile_advresnet_t_kernel(tc, x, y, beta, bias_lin, W1, W2, bias1, bias2, adv,
         y_v = y.rearrange("(p t) j -> p t j", t=NT)
         o_v = out.rearrange("(p t) j -> p t j", t=NT)
 
-        w2 = res.tile([P, NH], BF16, name="w2")
-        nc.scalar.dma_start(out=w2[:], in_=W2)
         brows = res.tile([P, N], BF16, name="brows")
         nc.vector.memset(brows[:], 0.0)
-        nc.scalar.dma_start(out=brows[0:1, :], in_=bias_lin.rearrange("(o n) -> o n", o=1))
-        nc.scalar.dma_start(out=brows[1:2, :], in_=bias2.rearrange("(o n) -> o n", o=1))
-
         braw = res.tile([P, 8 * N], BF16, name="braw")
-        nc.sync.dma_start(
-            out=braw[:].rearrange("p (g c) -> p g c", g=2),
-            in_=beta.rearrange("(g p t) j -> p g (t j)", g=2, p=P, t=4),
-        )
-        x_tiles = []
+        w2 = res.tile([P, NH], BF16, name="w2")
         x_of = []
         y_tiles = []
         s = 0
         for i, c in enumerate(X_CHUNKS):
-            for yi, b in enumerate(Y_BEFORE):
-                if b == i:
-                    y_sb = res.tile([P, 16 * N], BF16, name="y%d" % yi)
-                    nc.sync.dma_start(out=y_sb[:], in_=y_v[:, 16 * yi : 16 * yi + 16, :].rearrange("p t j -> p (t j)"))
-                    y_tiles.append(y_sb)
+            if i == BETA_AT:
+                nc.sync.dma_start(
+                    out=braw[:].rearrange("p (g c) -> p g c", g=2),
+                    in_=beta.rearrange("(g p t) j -> p g (t j)", g=2, p=P, t=4),
+                )
+            if i in Y_BEFORE:
+                yi = Y_BEFORE[i]
+                y_sb = res.tile([P, 16 * N], BF16, name="y%d" % yi)
+                nc.sync.dma_start(out=y_sb[:], in_=y_v[:, 16 * yi : 16 * yi + 16, :].rearrange("p t j -> p (t j)"))
+                y_tiles.append(y_sb)
             x_sb = res.tile([P, c * K], BF16, name="x%d" % i)
             nc.sync.dma_start(out=x_sb[:], in_=x_v[:, s : s + c, :].rearrange("p t k -> p (t k)"))
-            x_tiles.append(x_sb)
             for r in range(c):
-                x_of.append((i, r))
+                x_of.append(x_sb[:, r * K : (r + 1) * K])
             s += c
+            if i == BETA_AT:
+                nc.scalar.dma_start(out=w2[:], in_=W2)
+                nc.scalar.dma_start(out=brows[0:1, :], in_=bias_lin.rearrange("(o n) -> o n", o=1))
+                nc.scalar.dma_start(out=brows[1:2, :], in_=bias2.rearrange("(o n) -> o n", o=1))
         assert s == NT
 
         ident = res.tile([P, P], F32, name="ident")
@@ -83,57 +84,73 @@ def tile_advresnet_t_kernel(tc, x, y, beta, bias_lin, W1, W2, bias1, bias2, adv,
         nc.vector.memset(ones_f[:], 1.0)
         ones_b = res.tile([P, P], BF16, name="ones_b")
         nc.vector.memset(ones_b[:], 1.0)
-        warm = res.tile([P, 1], F32, name="warm")
-        nc.vector.memset(warm[:], 0.0)
-        nc.scalar.activation(out=warm[:], in_=warm[:], func=ACT.Abs)
 
-        absb = res.tile([P, 8 * N], BF16, name="absb")
-        nc.scalar.activation(out=absb[:], in_=braw[:], func=ACT.Abs)
-        w2junk = res.tile([P, NH], F32, name="w2junk")
-        w2s = res.tile([P, 1], F32, name="w2s")
-        nc.scalar.activation(out=w2junk[:], in_=w2[:], func=ACT.Copy, scale=float(NH), accum_out=w2s[:])
         bgrp = res.tile([P, 8 * N], BF16, name="bgrp", align_bytes=64)
         nc.vector.tensor_copy(
             out=bgrp[:].rearrange("p (g j t) -> p g j t", g=2, t=4),
             in_=braw[:].rearrange("p (g t j) -> p g j t", g=2, t=4),
         )
-        rhs_c = res.tile([P, N], F32, name="rhs_c")
-        nc.vector.scalar_tensor_tensor(
-            out=rhs_c[:], in0=ident[:], scalar=w2s[:, 0:1], in1=brows[:], op0=MULT, op1=ADD
+        absb = res.tile([P, 8 * N], BF16, name="absb")
+        nc.vector.scalar_tensor_tensor(out=absb[:], in0=braw[:], scalar=-1.0, in1=braw[:], op0=MULT, op1=MAX)
+        bcod = res.tile([P, 2 * N], U32, name="bcod", align_bytes=64)
+        bscl = res.tile([P, 2 * N], U8, name="bscl", align_bytes=64)
+        nc.vector.quantize_mx(out=bcod[:].bitcast(FP8X4), scales=bscl[:], in_=bgrp[:])
+        w2s = res.tile([P, 1], F32, name="w2s")
+        nc.vector.tensor_reduce(out=w2s[:], in_=w2[:], op=ADD, axis=AX)
+        diag = res.tile([P, P], F32, name="diag")
+        nc.vector.tensor_scalar(
+            out=diag[:], in0=ident[:], scalar1=w2s[:, 0:1], scalar2=float(NH), op0=MULT, op1=MULT
         )
+        rhs_c = res.tile([P, N], F32, name="rhs_c")
+        nc.vector.tensor_tensor(out=rhs_c[:], in0=diag[:], in1=brows[:], op=ADD)
         cst = ps_c.tile([P, GT * N], F32, name="cst")
-        for a in range(8):
-            nc.tensor.matmul(
-                out=cst[:, 0:N], lhsT=ones_b[:], rhs=absb[:, a * N : (a + 1) * N], start=(a == 0), stop=(a == 7)
-            )
         c_sb = res.tile([P, N], F32, name="c_sb")
+
+        def emit_cst():
+            for a in range(8):
+                nc.tensor.matmul(
+                    out=cst[:, 0:N], lhsT=ones_b[:], rhs=absb[:, a * N : (a + 1) * N], start=(a == 0), stop=(a == 7)
+                )
 
         def emit_c():
             c_ps = ps_o.tile([P, GT * N], F32, name="ops")
             nc.tensor.matmul(out=c_ps[:, 0:N], lhsT=ones_f[:], rhs=rhs_c[:], start=True, stop=True)
             nc.scalar.copy(out=c_sb[:], in_=c_ps[:, 0:N])
 
-        bcod = res.tile([P, 2 * N], U32, name="bcod", align_bytes=64)
-        bscl = res.tile([P, 2 * N], U8, name="bscl", align_bytes=64)
-        nc.vector.quantize_mx(out=bcod[:].bitcast(FP8X4), scales=bscl[:], in_=bgrp[:])
-
         grp_t = {}
         cod_t = {}
         ops_t = {}
-        o_chunks = [res.tile([P, 2 * GT * N], F32, name="o%d" % ci) for ci in range(NG // 2)]
-        o_tiles = [o_chunks[g // 2][:, (g % 2) * GT * N : (g % 2 + 1) * GT * N] for g in range(NG)]
-        add_eng = nc.gpsimd if ADD_ENGINE == "gpsimd" else nc.vector
+        perm_t = {}
+        o_sb = res.tile([P, NT * N], F32, name="o_sb")
+
+        def words_of(g):
+            return slice(STARTS[g] * N, (STARTS[g] + GROUPS[g]) * N)
+
+        def emit_perm(g):
+            if GROUPS[g] < GT or g == 0 or len(PERM) == 0:
+                return
+            n = len(PERM)
+            xp = perm_pool.tile([P, n * K], BF16, name="xp")
+            for q, tt in enumerate(PERM):
+                nc.vector.tensor_copy(
+                    out=xp[:, q * K : (q + 1) * K].bitcast(F32).rearrange("p (g u m) -> p g u m", g=2, u=2),
+                    in_=x_of[STARTS[g] + tt].bitcast(F32).rearrange("p (g m u) -> p g u m", g=2, u=2),
+                )
+                perm_t[STARTS[g] + tt] = xp[:, q * K : (q + 1) * K]
 
         def emit_transposes(g):
             grp = grp_pool.tile([P, GT * K], BF16, name="grp", align_bytes=64)
             grp_t[g] = grp
-            for tt in range(GT):
-                i, r = x_of[g * GT + tt]
-                xw = x_tiles[i][:, r * K : (r + 1) * K].bitcast(F32)
+            for tt in range(GROUPS[g]):
+                t = STARTS[g] + tt
                 xt = ps_x.tile([P, 4, P], F32, name="xt")
                 for w in range(4):
-                    g0 = (w // 2) * 2 * P
-                    nc.tensor.transpose(xt[:, w, :], xw[:, g0 + w % 2 : g0 + 2 * P : 2], ident[:])
+                    if t in perm_t:
+                        src = perm_t[t].bitcast(F32)[:, w * P : (w + 1) * P]
+                    else:
+                        h0 = (w // 2) * 2 * P
+                        src = x_of[t].bitcast(F32)[:, h0 + w % 2 : h0 + 2 * P : 2]
+                    nc.tensor.transpose(xt[:, w, :], src, ident[:])
                 dst = grp[:, tt * K : (tt + 1) * K].bitcast(F32).rearrange("p (g r u) -> p g r u", g=2, u=2)
                 nc.scalar.copy(out=dst, in_=xt[:].rearrange("p (g u) r -> p g r u", u=2))
 
@@ -141,20 +158,14 @@ def tile_advresnet_t_kernel(tc, x, y, beta, bias_lin, W1, W2, bias1, bias2, adv,
             cod = cod_pool.tile([P, GT * 2 * P], U32, name="cod", align_bytes=64)
             scl = cod_pool.tile([P, GT * 2 * P], U8, name="scl", align_bytes=64)
             cod_t[g] = (cod, scl)
-            parts = LAST_Q_PARTS if g == NG - 1 else 1
-            wq = GT * 2 * P // parts
-            for h in range(parts):
-                nc.vector.quantize_mx(
-                    out=cod[:, h * wq : (h + 1) * wq].bitcast(FP8X4),
-                    scales=scl[:, h * wq : (h + 1) * wq],
-                    in_=grp_t[g][:, 4 * h * wq : 4 * (h + 1) * wq],
-                )
+            wq = GROUPS[g] * 2 * P
+            nc.vector.quantize_mx(out=cod[:, 0:wq].bitcast(FP8X4), scales=scl[:, 0:wq], in_=grp_t[g][:, 0 : 4 * wq])
 
         def emit_mx(g):
             cod, scl = cod_t[g]
             ops = ps_o.tile([P, GT * N], F32, name="ops")
             ops_t[g] = ops
-            for tt in range(GT):
+            for tt in range(GROUPS[g]):
                 for h in range(2):
                     cs = slice((2 * tt + h) * P, (2 * tt + h + 1) * P)
                     nc.tensor.matmul_mx(
@@ -168,46 +179,57 @@ def tile_advresnet_t_kernel(tc, x, y, beta, bias_lin, W1, W2, bias1, bias2, adv,
                     )
 
         def emit_y_mul(g):
-            t0 = (g % 4) * GT
+            t0 = STARTS[g] % 16
             nc.vector.scalar_tensor_tensor(
-                out=o_tiles[g].rearrange("p (t j) -> p t j", j=N),
-                in0=y_tiles[g // 4][:, t0 * N : (t0 + GT) * N].rearrange("p (t j) -> p t j", j=N),
+                out=o_sb[:, words_of(g)].rearrange("p (t j) -> p t j", j=N),
+                in0=y_tiles[STARTS[g] // 16][:, t0 * N : (t0 + GROUPS[g]) * N].rearrange("p (t j) -> p t j", j=N),
                 scalar=-0.1,
-                in1=cst[:, 0:N].unsqueeze(1).to_broadcast([P, GT, N]),
+                in1=cst[:, 0:N].unsqueeze(1).to_broadcast([P, GROUPS[g], N]),
                 op0=MULT,
                 op1=MULT,
             )
 
         def emit_y_add(g):
-            o3 = o_tiles[g].rearrange("p (t j) -> p t j", j=N)
-            add_eng.tensor_tensor(out=o3, in0=o3, in1=c_sb[:].unsqueeze(1).to_broadcast([P, GT, N]), op=ADD)
+            o3 = o_sb[:, words_of(g)].rearrange("p (t j) -> p t j", j=N)
+            nc.gpsimd.tensor_tensor(
+                out=o3, in0=o3, in1=c_sb[:].unsqueeze(1).to_broadcast([P, GROUPS[g], N]), op=ADD
+            )
+
+        stored = [0]
 
         def emit_epilogue(g):
-            nc.vector.tensor_tensor(out=o_tiles[g], in0=ops_t[g][:], in1=o_tiles[g], op=ADD)
-            if g >= NG - 2:
-                nc.sync.dma_start(out=o_v[:, g * GT : (g + 1) * GT, :].rearrange("p t j -> p (t j)"), in_=o_tiles[g])
-            elif g % 2 == 1:
-                t0 = (g - 1) * GT
+            o_g = o_sb[:, words_of(g)]
+            nc.vector.tensor_tensor(out=o_g, in0=ops_t[g][:, 0 : GROUPS[g] * N], in1=o_g, op=ADD)
+            end = STARTS[g] + GROUPS[g]
+            if end - stored[0] >= 8 or g >= NG - 4:
+                t0 = stored[0]
                 nc.sync.dma_start(
-                    out=o_v[:, t0 : t0 + 2 * GT, :].rearrange("p t j -> p (t j)"), in_=o_chunks[g // 2][:]
+                    out=o_v[:, t0:end, :].rearrange("p t j -> p (t j)"), in_=o_sb[:, t0 * N : end * N]
                 )
+                stored[0] = end
 
-        for g in range(Y_HEAD):
-            emit_y_mul(g)
+        y_done = 0
         for g in range(NG + LAG_E):
             if g < NG:
                 emit_transposes(g)
             if g == 0:
+                emit_cst()
+            if g == 1:
                 emit_c()
-                for h in range(Y_HEAD):
-                    emit_y_add(h)
             if 0 <= g - LAG_M < NG:
                 emit_mx(g - LAG_M)
             if 0 <= g - LAG_E < NG:
                 emit_epilogue(g - LAG_E)
-            if g + Y_HEAD < NG:
-                emit_y_mul(g + Y_HEAD)
+            y_now = []
+            if g >= 1:
+                for k in range(Y_COUNT.get(g, 1)):
+                    if y_done < NG:
+                        emit_y_mul(y_done)
+                        y_now.append(y_done)
+                        y_done += 1
             if 0 <= g - LAG_Q < NG:
                 emit_quant(g - LAG_Q)
-            if g + Y_HEAD < NG:
-                emit_y_add(g + Y_HEAD)
+            if g + 1 < NG:
+                emit_perm(g + 1)
+            for h in y_now:
+                emit_y_add(h)

@@ -24,7 +24,7 @@ X_CHUNKS = [1, 1, 2] + [4] * 15
 Y_BEFORE = {2: 0, 5: 1, 8: 2, 11: 3}
 BETA_AT = 1
 GROUPS = [4] * 15 + [2, 1, 1]
-PERM = (3,)
+PERM = ()
 NG = len(GROUPS)
 STARTS = [sum(GROUPS[:g]) for g in range(NG)]
 LAG_Q, LAG_M, LAG_E = 1, 2, 3
@@ -191,7 +191,7 @@ def tile_advresnet_t_kernel(tc, x, y, beta, bias_lin, W1, W2, bias1, bias2, adv,
 
         def emit_y_add(g):
             o3 = o_sb[:, words_of(g)].rearrange("p (t j) -> p t j", j=N)
-            nc.gpsimd.tensor_tensor(
+            nc.vector.tensor_tensor(
                 out=o3, in0=o3, in1=c_sb[:].unsqueeze(1).to_broadcast([P, GROUPS[g], N]), op=ADD
             )
 

@@ -191,7 +191,7 @@ def tile_advresnet_t_kernel(tc, x, y, beta, bias_lin, W1, W2, bias1, bias2, adv,
 
         def emit_y_add(g):
             o3 = o_sb[:, words_of(g)].rearrange("p (t j) -> p t j", j=N)
-            nc.vector.tensor_tensor(
+            nc.gpsimd.tensor_tensor(
                 out=o3, in0=o3, in1=c_sb[:].unsqueeze(1).to_broadcast([P, GROUPS[g], N]), op=ADD
             )
 

@@ -24,7 +24,7 @@ X_CHUNKS = [1, 1, 2] + [4] * 15
 Y_BEFORE = {2: 0, 5: 1, 8: 2, 11: 3}
 BETA_AT = 1
 GROUPS = [4] * 15 + [2, 1, 1]
-PERM = ()
+PERM = (3,)
 NG = len(GROUPS)
 STARTS = [sum(GROUPS[:g]) for g in range(NG)]
 LAG_Q, LAG_M, LAG_E = 1, 2, 3
@@ -132,7 +132,7 @@ def tile_advresnet_t_kernel(tc, x, y, beta, bias_lin, W1, W2, bias1, bias2, adv,
             n = len(PERM)
             xp = perm_pool.tile([P, n * K], BF16, name="xp")
             for q, tt in enumerate(PERM):
-                nc.vector.tensor_copy(
+                nc.scalar.copy(
                     out=xp[:, q * K : (q + 1) * K].bitcast(F32).rearrange("p (g u m) -> p g u m", g=2, u=2),
                     in_=x_of[STARTS[g] + tt].bitcast(F32).rearrange("p (g m u) -> p g u m", g=2, u=2),
                 )

@@ -10,7 +10,6 @@ U8 = mybir.dt.uint8
 FP8X4 = mybir.dt.float8_e4m3fn_x4
 ADD = mybir.AluOpType.add
 MULT = mybir.AluOpType.mult
-MAX = mybir.AluOpType.max
 AX = mybir.AxisListType.X
 
 P = 128
@@ -20,16 +19,16 @@ GT = 4
 FLOPS = 2 * B * K * N
 BYTES = 2 * (B * K + B * N + K * N + N * NH + 2 * N) + 4 * B * N
 
-X_CHUNKS = [1, 1, 2] + [4] * 15
-Y_BEFORE = {2: 0, 5: 1, 8: 2, 11: 3}
-BETA_AT = 1
+X_CHUNKS = [1, 1, 1, 1, 2, 2] + [4] * 14
+Y_BEFORE = {6: 0, 9: 1, 13: 2, 16: 3}
+BETA_AT = 4
 GROUPS = [4] * 15 + [2, 1, 1]
 PERM = (3,)
 NG = len(GROUPS)
 STARTS = [sum(GROUPS[:g]) for g in range(NG)]
 LAG_Q, LAG_M, LAG_E = 1, 2, 3
 XT_BUFS = 5
-Y_COUNT = {1: 2, 2: 2}
+Y_COUNT = {1: 0, 2: 2, 3: 2}
 
 
 def tile_advresnet_t_kernel(tc, x, y, beta, bias_lin, W1, W2, bias1, bias2, adv, out):
@@ -82,16 +81,12 @@ def tile_advresnet_t_kernel(tc, x, y, beta, bias_lin, W1, W2, bias1, bias2, adv,
         make_identity(nc, ident[:])
         ones_f = res.tile([P, P], F32, name="ones_f")
         nc.vector.memset(ones_f[:], 1.0)
-        ones_b = res.tile([P, P], BF16, name="ones_b")
-        nc.vector.memset(ones_b[:], 1.0)
 
         bgrp = res.tile([P, 8 * N], BF16, name="bgrp", align_bytes=64)
         nc.vector.tensor_copy(
             out=bgrp[:].rearrange("p (g j t) -> p g j t", g=2, t=4),
             in_=braw[:].rearrange("p (g t j) -> p g j t", g=2, t=4),
         )
-        absb = res.tile([P, 8 * N], BF16, name="absb")
-        nc.vector.scalar_tensor_tensor(out=absb[:], in0=braw[:], scalar=-1.0, in1=braw[:], op0=MULT, op1=MAX)
         bcod = res.tile([P, 2 * N], U32, name="bcod", align_bytes=64)
         bscl = res.tile([P, 2 * N], U8, name="bscl", align_bytes=64)
         nc.vector.quantize_mx(out=bcod[:].bitcast(FP8X4), scales=bscl[:], in_=bgrp[:])
@@ -101,21 +96,19 @@ def tile_advresnet_t_kernel(tc, x, y, beta, bias_lin, W1, W2, bias1, bias2, adv,
         nc.vector.tensor_scalar(
             out=diag[:], in0=ident[:], scalar1=w2s[:, 0:1], scalar2=float(NH), op0=MULT, op1=MULT
         )
-        rhs_c = res.tile([P, N], F32, name="rhs_c")
-        nc.vector.tensor_tensor(out=rhs_c[:], in0=diag[:], in1=brows[:], op=ADD)
+        nsum = res.tile([P, 2 * N], F32, name="nsum")
+        nc.vector.tensor_reduce(
+            out=nsum[:], in_=bgrp[:].rearrange("p (c t) -> p c t", t=4), op=ADD, axis=AX, apply_absolute_value=True
+        )
+        rhs = res.tile([P, 2 * N], F32, name="rhs")
+        nc.vector.tensor_tensor(out=rhs[:, N : 2 * N], in0=diag[:], in1=brows[:], op=ADD)
+        nc.vector.tensor_tensor(out=rhs[:, 0:N], in0=nsum[:, 0:N], in1=nsum[:, N : 2 * N], op=ADD)
         cst = ps_c.tile([P, GT * N], F32, name="cst")
         c_sb = res.tile([P, N], F32, name="c_sb")
 
         def emit_cst():
-            for a in range(8):
-                nc.tensor.matmul(
-                    out=cst[:, 0:N], lhsT=ones_b[:], rhs=absb[:, a * N : (a + 1) * N], start=(a == 0), stop=(a == 7)
-                )
-
-        def emit_c():
-            c_ps = ps_o.tile([P, GT * N], F32, name="ops")
-            nc.tensor.matmul(out=c_ps[:, 0:N], lhsT=ones_f[:], rhs=rhs_c[:], start=True, stop=True)
-            nc.scalar.copy(out=c_sb[:], in_=c_ps[:, 0:N])
+            nc.tensor.matmul(out=cst[:, 0 : 2 * N], lhsT=ones_f[:], rhs=rhs[:], start=True, stop=True)
+            nc.scalar.copy(out=c_sb[:], in_=cst[:, N : 2 * N])
 
         grp_t = {}
         cod_t = {}
@@ -127,7 +120,7 @@ def tile_advresnet_t_kernel(tc, x, y, beta, bias_lin, W1, W2, bias1, bias2, adv,
             return slice(STARTS[g] * N, (STARTS[g] + GROUPS[g]) * N)
 
         def emit_perm(g):
-            if GROUPS[g] < GT or g == 0 or len(PERM) == 0:
+            if GROUPS[g] < GT or g % 2 == 0 or len(PERM) == 0:
                 return
             n = len(PERM)
             xp = perm_pool.tile([P, n * K], BF16, name="xp")
@@ -212,10 +205,8 @@ def tile_advresnet_t_kernel(tc, x, y, beta, bias_lin, W1, W2, bias1, bias2, adv,
         for g in range(NG + LAG_E):
             if g < NG:
                 emit_transposes(g)
-            if g == 0:
-                emit_cst()
             if g == 1:
-                emit_c()
+                emit_cst()
             if 0 <= g - LAG_M < NG:
                 emit_mx(g - LAG_M)
             if 0 <= g - LAG_E < NG:

from contextlib import ExitStack

import concourse.mybir as mybir
from concourse.masks import make_identity

F32 = mybir.dt.float32
BF16 = mybir.dt.bfloat16
U32 = mybir.dt.uint32
U8 = mybir.dt.uint8
FP8X4 = mybir.dt.float8_e4m3fn_x4
ADD = mybir.AluOpType.add
MULT = mybir.AluOpType.mult
AX = mybir.AxisListType.X

P = 128
B, K, N, NH = 8192, 1024, 128, 512
NT = B // P
GT = 4
FLOPS = 2 * B * K * N
BYTES = 2 * (B * K + B * N + K * N + N * NH + 2 * N) + 4 * B * N

X_CHUNKS = [1, 1, 1, 1, 2, 2] + [4] * 14
Y_BEFORE = {6: 0, 9: 1, 13: 2, 16: 3}
BETA_AT = 4
GROUPS = [4] * 15 + [2, 1, 1]
PERM = (3,)
NG = len(GROUPS)
STARTS = [sum(GROUPS[:g]) for g in range(NG)]
LAG_Q, LAG_M, LAG_E = 1, 2, 3
XT_BUFS = 5
Y_COUNT = {1: 0, 2: 2, 3: 2}


def tile_advresnet_t_kernel(tc, x, y, beta, bias_lin, W1, W2, bias1, bias2, adv, out):
    assert adv == 1
    nc = tc.nc
    with ExitStack() as ctx:
        ctx.enter_context(tc.manual_schedule())
        res = ctx.enter_context(tc.tile_pool(name="res", bufs=1))
        grp_pool = ctx.enter_context(tc.tile_pool(name="grp", bufs=3))
        cod_pool = ctx.enter_context(tc.tile_pool(name="cod", bufs=3))
        perm_pool = ctx.enter_context(tc.tile_pool(name="perm", bufs=3))
        ps_c = ctx.enter_context(tc.psum_pool(name="psc", bufs=1))
        ps_x = ctx.enter_context(tc.psum_pool(name="psx", bufs=XT_BUFS))
        ps_o = ctx.enter_context(tc.psum_pool(name="pso", bufs=7 - XT_BUFS))

        x_v = x.rearrange("(p t) k -> p t k", t=NT)
        y_v = y.rearrange("(p t) j -> p t j", t=NT)
        o_v = out.rearrange("(p t) j -> p t j", t=NT)

        brows = res.tile([P, N], BF16, name="brows")
        nc.vector.memset(brows[:], 0.0)
        braw = res.tile([P, 8 * N], BF16, name="braw")
        w2 = res.tile([P, NH], BF16, name="w2")
        x_of = []
        y_tiles = []
        s = 0
        for i, c in enumerate(X_CHUNKS):
            if i == BETA_AT:
                nc.sync.dma_start(
                    out=braw[:].rearrange("p (g c) -> p g c", g=2),
                    in_=beta.rearrange("(g p t) j -> p g (t j)", g=2, p=P, t=4),
                )
            if i in Y_BEFORE:
                yi = Y_BEFORE[i]
                y_sb = res.tile([P, 16 * N], BF16, name="y%d" % yi)
                nc.sync.dma_start(out=y_sb[:], in_=y_v[:, 16 * yi : 16 * yi + 16, :].rearrange("p t j -> p (t j)"))
                y_tiles.append(y_sb)
            x_sb = res.tile([P, c * K], BF16, name="x%d" % i)
            nc.sync.dma_start(out=x_sb[:], in_=x_v[:, s : s + c, :].rearrange("p t k -> p (t k)"))
            for r in range(c):
                x_of.append(x_sb[:, r * K : (r + 1) * K])
            s += c
            if i == BETA_AT:
                nc.scalar.dma_start(out=w2[:], in_=W2)
                nc.scalar.dma_start(out=brows[0:1, :], in_=bias_lin.rearrange("(o n) -> o n", o=1))
                nc.scalar.dma_start(out=brows[1:2, :], in_=bias2.rearrange("(o n) -> o n", o=1))
        assert s == NT

        ident = res.tile([P, P], F32, name="ident")
        make_identity(nc, ident[:])
        ones_f = res.tile([P, P], F32, name="ones_f")
        nc.vector.memset(ones_f[:], 1.0)

        bgrp = res.tile([P, 8 * N], BF16, name="bgrp", align_bytes=64)
        nc.vector.tensor_copy(
            out=bgrp[:].rearrange("p (g j t) -> p g j t", g=2, t=4),
            in_=braw[:].rearrange("p (g t j) -> p g j t", g=2, t=4),
        )
        bcod = res.tile([P, 2 * N], U32, name="bcod", align_bytes=64)
        bscl = res.tile([P, 2 * N], U8, name="bscl", align_bytes=64)
        nc.vector.quantize_mx(out=bcod[:].bitcast(FP8X4), scales=bscl[:], in_=bgrp[:])
        w2s = res.tile([P, 1], F32, name="w2s")
        nc.vector.tensor_reduce(out=w2s[:], in_=w2[:], op=ADD, axis=AX)
        diag = res.tile([P, P], F32, name="diag")
        nc.vector.tensor_scalar(
            out=diag[:], in0=ident[:], scalar1=w2s[:, 0:1], scalar2=float(NH), op0=MULT, op1=MULT
        )
        nsum = res.tile([P, 2 * N], F32, name="nsum")
        nc.vector.tensor_reduce(
            out=nsum[:], in_=bgrp[:].rearrange("p (c t) -> p c t", t=4), op=ADD, axis=AX, apply_absolute_value=True
        )
        rhs = res.tile([P, 2 * N], F32, name="rhs")
        nc.vector.tensor_tensor(out=rhs[:, N : 2 * N], in0=diag[:], in1=brows[:], op=ADD)
        nc.vector.tensor_tensor(out=rhs[:, 0:N], in0=nsum[:, 0:N], in1=nsum[:, N : 2 * N], op=ADD)
        cst = ps_c.tile([P, GT * N], F32, name="cst")
        c_sb = res.tile([P, N], F32, name="c_sb")

        def emit_cst():
            nc.tensor.matmul(out=cst[:, 0 : 2 * N], lhsT=ones_f[:], rhs=rhs[:], start=True, stop=True)
            nc.scalar.copy(out=c_sb[:], in_=cst[:, N : 2 * N])

        grp_t = {}
        cod_t = {}
        ops_t = {}
        perm_t = {}
        o_sb = res.tile([P, NT * N], F32, name="o_sb")

        def words_of(g):
            return slice(STARTS[g] * N, (STARTS[g] + GROUPS[g]) * N)

        def emit_perm(g):
            if GROUPS[g] < GT or g % 2 == 0 or len(PERM) == 0:
                return
            n = len(PERM)
            xp = perm_pool.tile([P, n * K], BF16, name="xp")
            for q, tt in enumerate(PERM):
                nc.scalar.copy(
                    out=xp[:, q * K : (q + 1) * K].bitcast(F32).rearrange("p (g u m) -> p g u m", g=2, u=2),
                    in_=x_of[STARTS[g] + tt].bitcast(F32).rearrange("p (g m u) -> p g u m", g=2, u=2),
                )
                perm_t[STARTS[g] + tt] = xp[:, q * K : (q + 1) * K]

        def emit_transposes(g):
            grp = grp_pool.tile([P, GT * K], BF16, name="grp", align_bytes=64)
            grp_t[g] = grp
            for tt in range(GROUPS[g]):
                t = STARTS[g] + tt
                xt = ps_x.tile([P, 4, P], F32, name="xt")
                for w in range(4):
                    if t in perm_t:
                        src = perm_t[t].bitcast(F32)[:, w * P : (w + 1) * P]
                    else:
                        h0 = (w // 2) * 2 * P
                        src = x_of[t].bitcast(F32)[:, h0 + w % 2 : h0 + 2 * P : 2]
                    nc.tensor.transpose(xt[:, w, :], src, ident[:])
                dst = grp[:, tt * K : (tt + 1) * K].bitcast(F32).rearrange("p (g r u) -> p g r u", g=2, u=2)
                nc.scalar.copy(out=dst, in_=xt[:].rearrange("p (g u) r -> p g r u", u=2))

        def emit_quant(g):
            cod = cod_pool.tile([P, GT * 2 * P], U32, name="cod", align_bytes=64)
            scl = cod_pool.tile([P, GT * 2 * P], U8, name="scl", align_bytes=64)
            cod_t[g] = (cod, scl)
            wq = GROUPS[g] * 2 * P
            nc.vector.quantize_mx(out=cod[:, 0:wq].bitcast(FP8X4), scales=scl[:, 0:wq], in_=grp_t[g][:, 0 : 4 * wq])

        def emit_mx(g):
            cod, scl = cod_t[g]
            ops = ps_o.tile([P, GT * N], F32, name="ops")
            ops_t[g] = ops
            for tt in range(GROUPS[g]):
                for h in range(2):
                    cs = slice((2 * tt + h) * P, (2 * tt + h + 1) * P)
                    nc.tensor.matmul_mx(
                        out=ops[:, tt * N : (tt + 1) * N],
                        lhsT=cod[:, cs].bitcast(FP8X4),
                        lhsT_scale=scl[:, cs],
                        rhs=bcod[:, h * N : (h + 1) * N].bitcast(FP8X4),
                        rhs_scale=bscl[:, h * N : (h + 1) * N],
                        start=(h == 0),
                        stop=(h == 1),
                    )

        def emit_y_mul(g):
            t0 = STARTS[g] % 16
            nc.vector.scalar_tensor_tensor(
                out=o_sb[:, words_of(g)].rearrange("p (t j) -> p t j", j=N),
                in0=y_tiles[STARTS[g] // 16][:, t0 * N : (t0 + GROUPS[g]) * N].rearrange("p (t j) -> p t j", j=N),
                scalar=-0.1,
                in1=cst[:, 0:N].unsqueeze(1).to_broadcast([P, GROUPS[g], N]),
                op0=MULT,
                op1=MULT,
            )

        def emit_y_add(g):
            o3 = o_sb[:, words_of(g)].rearrange("p (t j) -> p t j", j=N)
            nc.gpsimd.tensor_tensor(
                out=o3, in0=o3, in1=c_sb[:].unsqueeze(1).to_broadcast([P, GROUPS[g], N]), op=ADD
            )

        stored = [0]

        def emit_epilogue(g):
            o_g = o_sb[:, words_of(g)]
            nc.vector.tensor_tensor(out=o_g, in0=ops_t[g][:, 0 : GROUPS[g] * N], in1=o_g, op=ADD)
            end = STARTS[g] + GROUPS[g]
            if end - stored[0] >= 8 or g >= NG - 4:
                t0 = stored[0]
                nc.sync.dma_start(
                    out=o_v[:, t0:end, :].rearrange("p t j -> p (t j)"), in_=o_sb[:, t0 * N : end * N]
                )
                stored[0] = end

        y_done = 0
        for g in range(NG + LAG_E):
            if g < NG:
                emit_transposes(g)
            if g == 1:
                emit_cst()
            if 0 <= g - LAG_M < NG:
                emit_mx(g - LAG_M)
            if 0 <= g - LAG_E < NG:
                emit_epilogue(g - LAG_E)
            y_now = []
            if g >= 1:
                for k in range(Y_COUNT.get(g, 1)):
                    if y_done < NG:
                        emit_y_mul(y_done)
                        y_now.append(y_done)
                        y_done += 1
            if 0 <= g - LAG_Q < NG:
                emit_quant(g - LAG_Q)
            if g + 1 < NG:
                emit_perm(g + 1)
            for h in y_now:
                emit_y_add(h)
